import numpy as np
import ml_dtypes


def mxq(x, axis, fmt="e4m3"):
    dtype, down = {"e4m3": (ml_dtypes.float8_e4m3fn, 7), "e5m2": (ml_dtypes.float8_e5m2, 14)}[fmt]
    v = np.moveaxis(np.asarray(x, np.float32).astype(ml_dtypes.bfloat16).astype(np.float64), axis, -1)
    blocks = v.reshape(v.shape[:-1] + (-1, 32))
    amax = np.abs(blocks).max(-1, keepdims=True)
    byte = np.maximum(np.where(amax > 0, np.frexp(amax)[1] - 1 + 127, 0) - down, 1)
    scale = np.exp2(byte - 127.0)
    codes = (blocks / scale).astype(np.float32).astype(dtype).astype(np.float64)
    return np.moveaxis((codes * scale).reshape(v.shape), -1, axis)


WIDE = False


def mx_kscale(k):
    if not WIDE:
        return np.ones(k)
    levels = np.array([10, -10, 5, -5, 0])
    if k % 512:
        return np.exp2(np.random.permutation(np.resize(levels, k // 32))).repeat(32)
    a = np.empty((k // 512, 16))
    for p in range(k // 512):
        a[p, :8] = np.random.permutation(np.resize(levels, 8))
        for g in range(8):
            far = levels[np.abs(levels - a[p, g]) >= 10]
            a[p, g + 8] = far[np.random.randint(len(far))]
    return np.exp2(a.ravel()).repeat(32)


BF16 = ml_dtypes.bfloat16


def bf(x):
    return np.asarray(x, np.float32).astype(BF16)


def f64(x):
    return np.asarray(x).astype(np.float64)


E2M1 = np.array([0.0, 0.5, 1.0, 1.5, 2.0, 3.0, 4.0, 6.0, -0.0, -0.5, -1.0, -1.5, -2.0, -3.0, -4.0, -6.0])


def pack_weight(w, fmt):
    k, n = w.shape
    w = f64(bf(w)).reshape(k // 32, 32, n)
    amax = np.abs(w).max(1)
    if fmt == "e4m3":
        byte = np.frexp(amax)[1] - 1 + 127 - 7
    else:
        mant, ex = np.frexp(amax / 6.0)
        byte = np.where(mant > 0.5, ex, ex - 1) + 127
    byte = np.clip(np.where(amax > 0, byte, 1), 1, 254)
    scaled = (w * np.exp2(127.0 - byte)[:, None, :]).reshape(k, n).astype(np.float32)
    by_word = np.ascontiguousarray(scaled.reshape(k // 512, 128, 4, n).transpose(0, 1, 3, 2))
    if fmt == "e4m3":
        words = by_word.astype(ml_dtypes.float8_e4m3fn).view(np.uint8)
    else:
        c = by_word.astype(ml_dtypes.float4_e2m1fn).view(np.uint8) & 0xF
        words = c[..., 0::2] | (c[..., 1::2] << 4)
    return np.ascontiguousarray(words), np.ascontiguousarray(byte.astype(np.uint8).reshape(k // 512, 16, n))


def unpack_weight(words, scales, fmt):
    g, p, n, _ = words.shape
    if fmt == "e4m3":
        vals = np.ascontiguousarray(words).view(ml_dtypes.float8_e4m3fn).astype(np.float64)
    else:
        nib = np.empty((g, p, n, 4), np.uint8)
        nib[..., 0::2] = words & 0xF
        nib[..., 1::2] = words >> 4
        vals = E2M1[nib]
    vals = vals * np.repeat(np.exp2(scales.astype(np.float64) - 127.0), 8, axis=1)[..., None]
    return vals.transpose(0, 1, 3, 2).reshape(g * 512, n)
def pack4(w):
    words, scales = pack_weight(w, "e2m1")
    return words.reshape(words.shape[0], 128, -1), scales


def unpack4(words, scales):
    return unpack_weight(words.reshape(words.shape[0], 128, -1, 2), scales, "e2m1")


B, N, F, DIM, H, DH, D3 = 4, 196, 16, 512, 1, 64, 512
W = H * D3
SCALE = 1.0 / (np.sqrt(DH) * H)
QS = np.sqrt(1.5 / (SCALE * np.sqrt(D3)))


def draw0():
    s, t = mx_kscale(DIM), mx_kscale(D3)
    th = np.tile(t, H)
    x = bf(np.random.standard_normal((B, N * F, DIM)) * s)
    words, scales = pack4(np.random.standard_normal((DIM, W)) * QS / np.sqrt(DIM) / s[:, None] * th)
    return {"x": x,
            "Wq_words": words,
            "Wq_scales": scales,
            "bq": bf(np.random.standard_normal(W) * 0.2 * QS * th),
            "k": bf(np.random.standard_normal((B, H, N, F, D3)) * QS / t)}


def core(x, Wq_words, Wq_scales, bq, k):
    y = (mxq(f64(x), 2, "e4m3") @ unpack4(Wq_words, Wq_scales)) + f64(bq)
    q = y.reshape(B, F, N, H, D3).transpose(0, 3, 2, 1, 4)
    s = (mxq(q, 4, "e4m3") @ mxq(f64(k), 4, "e4m3").transpose(0, 1, 2, 4, 3)) * SCALE
    e = np.exp(s - s.max(-1, keepdims=True))
    return e / e.sum(-1, keepdims=True)


def e4m3fn_bytes(y):
    return np.clip(np.asarray(y, np.float64), -448.0, 448.0).astype(np.float32).astype(ml_dtypes.float8_e4m3fn).view(np.uint8)


def e4m3fn_values(b):
    return np.asarray(b, np.uint8).view(ml_dtypes.float8_e4m3fn).astype(np.float64)


def setup_inputs():
    d = draw0()
    x0 = np.asarray(d['x']).astype(np.float64)
    s = (np.max(np.abs(x0), axis=(0, 1), keepdims=True) / 448.0).astype(np.float32)
    out = {}
    for k, v in d.items():
        if k == 'x':
            out['x_bytes'] = e4m3fn_bytes(x0 / s.astype(np.float64))
            out['x_scale'] = s
        else:
            out[k] = v
    return out


def reference(x_bytes, x_scale, Wq_words, Wq_scales, bq, k):
    return core(e4m3fn_values(x_bytes) * x_scale.astype(np.float64), Wq_words, Wq_scales, bq, k)

@@ -1,0 +1,301 @@
+from contextlib import ExitStack
+
+import concourse.mybir as mybir
+from concourse.masks import make_identity
+
+B, N, F, D = 4, 196, 16, 512
+ROWS = B * N * F
+FLOPS = 2 * ROWS * D * D + 2 * ROWS * F * D
+
+F32 = mybir.dt.float32
+BF16 = mybir.dt.bfloat16
+I32 = mybir.dt.int32
+U32 = mybir.dt.uint32
+U8 = mybir.dt.uint8
+FP8 = mybir.dt.float8_e4m3fn
+FP8X4 = mybir.dt.float8_e4m3fn_x4
+FP4X4 = mybir.dt.float4_e2m1fn_x4
+ACT = mybir.ActivationFunctionType
+ALU = mybir.AluOpType
+AX = mybir.AxisListType
+
+P = 128
+HALF = 98
+UNITS = HALF // 2
+X_CHUNKS = [2] + [8] * 12
+K_CHUNKS = [2, 4, 8] + [14] * 6
+BATCH = 16
+
+
+def is_direct(i):
+    return i % 4 == 3
+
+
+def tile_dividedspacetimeattention_pa_t_w4_kernel(tc, x_bytes, x_scale, Wq_words, Wq_scales, bq, k, out):
+    nc = tc.nc
+    with ExitStack() as ctx:
+        const = ctx.enter_context(tc.tile_pool(name="const", bufs=1))
+        big = ctx.enter_context(tc.tile_pool(name="big", bufs=1))
+        work = ctx.enter_context(tc.tile_pool(name="work", bufs=3))
+        codes = ctx.enter_context(tc.tile_pool(name="codes", bufs=5))
+        soft = ctx.enter_context(tc.tile_pool(name="soft", bufs=2))
+        outs = ctx.enter_context(tc.tile_pool(name="outs", bufs=4))
+        ps_t = ctx.enter_context(tc.psum_pool(name="ps_t", bufs=2))
+        ps_y = ctx.enter_context(tc.psum_pool(name="ps_y", bufs=3))
+        ps_s = ctx.enter_context(tc.psum_pool(name="ps_s", bufs=1))
+        ctx.enter_context(tc.manual_schedule())
+
+        ident = const.tile([P, P], F32, name="ident")
+        make_identity(nc, ident[:])
+        ws_raw = const.tile([P, D], U8, name="ws_raw", align_bytes=64)
+        nc.gpsimd.memset(ws_raw[:].bitcast(I32), 0)
+
+        x_rows = x_bytes.rearrange("b (q j) d -> (b q) (j d)", j=HALF)
+        x_tiles = []
+        for c, n in enumerate(X_CHUNKS):
+            x_tiles.append(big.tile([P, n * D], U8, name=f"x8_{c}", align_bytes=64))
+        k_view = k.rearrange("b o (h j) g d -> (b o h) g j d", j=HALF)
+        k_tiles = []
+        for c, n in enumerate(K_CHUNKS):
+            k_tiles.append(big.tile([P, n, D], BF16, name=f"kraw_{c}", align_bytes=64))
+        x_at, k_at = [], []
+        for c, n in enumerate(X_CHUNKS):
+            x_at += [(c, o) for o in range(n)]
+        for c, n in enumerate(K_CHUNKS):
+            k_at += [(c, o) for o in range(n)]
+
+        def load_x(c):
+            o = sum(X_CHUNKS[:c]) * D
+            nc.sync.dma_start(out=x_tiles[c][:], in_=x_rows[:, o : o + X_CHUNKS[c] * D])
+
+        def load_k(c):
+            o = sum(K_CHUNKS[:c])
+            for q in range(8):
+                nc.sync.dma_start(out=k_tiles[c][16 * q : 16 * q + 16, :, :], in_=k_view[q, :, o : o + K_CHUNKS[c], :])
+
+        scale = const.tile([P, 2 * D], F32, name="scale", align_bytes=64)
+        bq_raw = const.tile([P, 4], BF16, name="bq_raw")
+        w_raw = const.tile([P, 2 * D], U8, name="w_raw", align_bytes=64)
+        w_perm = const.tile([P, 2 * D], U8, name="w_perm", align_bytes=64)
+        ws_perm = const.tile([P, D], U8, name="ws_perm", align_bytes=64)
+        bqf = const.tile([P, 4], F32, name="bqf")
+        pick = const.tile([P, 2], F32, name="pick")
+
+        load_x(0)
+        nc.sync.dma_start(out=scale[:, 0:D], in_=x_scale.rearrange("a b k -> (a b k)").partition_broadcast(P))
+        load_k(0)
+        nc.sync.dma_start(out=w_raw[:], in_=Wq_words[0])
+        for q in range(4):
+            nc.sync.dma_start(out=ws_raw[32 * q : 32 * q + 4, :].bitcast(I32), in_=Wq_scales[0, 4 * q : 4 * q + 4, :].bitcast(I32))
+        nc.sync.dma_start(out=bq_raw[:], in_=bq.rearrange("(p t) -> p t", t=4))
+        load_x(1)
+        load_k(1)
+        load_k(2)
+        load_x(2)
+        nx = 3
+        for c in range(3, len(K_CHUNKS)):
+            load_k(c)
+            for r in range(2):
+                if nx < len(X_CHUNKS):
+                    load_x(nx)
+                    nx += 1
+
+        warm = const.tile([P, 1], F32, name="warm")
+        nc.scalar.activation(out=warm[:], in_=ident[:, 0:1], func=ACT.Exp)
+        nc.scalar.copy(out=scale[:, D : 2 * D], in_=scale[:, 0:D])
+
+        xb, xk_of, c_of, cs_of, yb_of, qp_of, qg_of, qc_of, qcs_of, t_of = {}, {}, {}, {}, {}, {}, {}, {}, {}, {}
+
+        def scale_x(i):
+            t = work.tile([P, 2 * D], BF16, name="xb", align_bytes=64)
+            c, o = x_at[2 * i]
+            nc.vector.tensor_tensor(out=t[:], in0=x_tiles[c][:, o * D : (o + 2) * D].bitcast(FP8), in1=scale[:], op=ALU.mult)
+            xb[i] = t
+
+        def scale_x_first():
+            t = work.tile([P, 2 * D], BF16, name="xb", align_bytes=64)
+            for a in range(2):
+                nc.vector.tensor_tensor(out=t[:, a * D : (a + 1) * D], in0=x_tiles[0][:, a * D : (a + 1) * D].bitcast(FP8), in1=scale[:, 0:D], op=ALU.mult)
+            xb[0] = t
+
+        def transposes(i):
+            tx = ps_t.tile([P, 2, 2, P], F32, name="tx")
+            tk = ps_t.tile([P, 2, 2, P], F32, name="tk")
+            words = xb.pop(i)[:].bitcast(F32)
+            for a in range(2):
+                for u in range(2):
+                    nc.tensor.transpose(tx[:, a, u, :], words[:, 256 * a + u : 256 * (a + 1) : 2], ident[:])
+            for a in range(2):
+                c, o = k_at[2 * i + a]
+                kw = k_tiles[c][:, o, :].bitcast(F32)
+                for u in range(2):
+                    nc.tensor.transpose(tk[:, a, u, :], kw[:, u:256:2], ident[:])
+            t_of[i] = (tx, tk)
+
+        def copies(i):
+            xk = work.tile([P, 2, 1024], BF16, name="xk", align_bytes=64)
+            for s, t in enumerate(t_of.pop(i)):
+                nc.scalar.copy(out=xk[:, s, :].bitcast(F32).rearrange("p (a r u) -> p a r u", a=2, u=2), in_=t[:].rearrange("p a u r -> p a r u"))
+            xk_of[i] = xk
+
+        def quant_xk(i):
+            c = codes.tile([P, 512], U32, name="xk_codes", align_bytes=64)
+            s = codes.tile([P, 512], U8, name="xk_scales", align_bytes=64)
+            nc.vector.quantize_mx(out=c[:].bitcast(FP8X4), scales=s[:], in_=xk_of.pop(i)[:].rearrange("p s n -> p (s n)"))
+            c_of[i], cs_of[i] = c, s
+
+        def w_cols(t):
+            return dict(lhsT=w_perm[:, 256 * t : 256 * t + 256].bitcast(FP4X4), lhsT_scale=ws_perm[:, 128 * t : 128 * t + 128])
+
+        def project(i):
+            c, s = c_of[i], cs_of[i]
+            banks = []
+            for h in range(2):
+                if is_direct(i):
+                    yb = ps_y.tile([P, 4, P], F32, name="yb")
+                    for t in range(4):
+                        nc.tensor.matmul_mx(out=yb[:, t, :], rhs=c[:, P * h : P * h + P].bitcast(FP8X4), rhs_scale=s[:, P * h : P * h + P], start=True, stop=True, **w_cols(t))
+                else:
+                    yb = ps_y.tile([P, 2, 2 * P], F32, name="yb")
+                    for e in range(2):
+                        nc.tensor.matmul_mx(out=yb[:, e, :], rhs=c[:, 0:256].bitcast(FP8X4), rhs_scale=s[:, 0:256], start=True, stop=True, **w_cols(2 * h + e))
+                banks.append(yb)
+            yb_of[i] = banks
+
+        def bias_pairs(i):
+            qp = work.tile([P, 2, 256, 2], BF16, name="qp", align_bytes=64)
+            for u, yb in enumerate(yb_of.pop(i)):
+                for e in range(2):
+                    t = 2 * u + e
+                    nc.scalar.activation(out=qp[:, u, :, e], in_=yb[:, e, :], func=ACT.Identity, bias=bqf[:, t : t + 1], scale=1.0)
+            qp_of[i] = qp
+
+        def weave(i):
+            qg = work.tile([P, 256, 4], BF16, name="qg", align_bytes=64)
+            nc.vector.tensor_copy(
+                out=qg[:].rearrange("p n t -> p (n t)").bitcast(F32).rearrange("p (n u) -> p n u", u=2),
+                in_=qp_of.pop(i)[:].rearrange("p u n e -> p (u n e)").bitcast(F32).rearrange("p (u n) -> p n u", u=2),
+            )
+            qg_of[i] = qg
+
+        def bias_direct(i):
+            qg = work.tile([P, 256, 4], BF16, name="qg", align_bytes=64)
+            for h, yb in enumerate(yb_of.pop(i)):
+                nc.vector.tensor_tensor(out=qg[:, P * h : P * h + P, :], in0=yb[:].rearrange("p t n -> p n t"), in1=bqf[:].unsqueeze(1).to_broadcast([P, P, 4]), op=ALU.add)
+            qg_of[i] = qg
+
+        def quant_q(i):
+            c = codes.tile([P, 256], U32, name="q_codes", align_bytes=64)
+            s = codes.tile([P, 256], U8, name="q_scales", align_bytes=64)
+            nc.vector.quantize_mx(out=c[:].bitcast(FP8X4), scales=s[:], in_=qg_of.pop(i)[:].rearrange("p n t -> p (n t)"))
+            qc_of[i], qcs_of[i] = c, s
+
+        state = {}
+
+        def scores(i):
+            if i % 2 == 0:
+                state["s"] = ps_s.tile([P, 4, P], F32, name="sb")
+            sb = state["s"]
+            qc, qs, kc, ks = qc_of.pop(i), qcs_of.pop(i), c_of.pop(i), cs_of.pop(i)
+            for a in range(2):
+                q_cols = slice(P * a, P * a + P)
+                k_cols = slice(256 + P * a, 256 + P * a + P)
+                nc.tensor.matmul_mx(out=sb[:, 2 * (i % 2) + a, :], lhsT=qc[:, q_cols].bitcast(FP8X4), lhsT_scale=qs[:, q_cols], rhs=kc[:, k_cols].bitcast(FP8X4), rhs_scale=ks[:, k_cols], start=True, stop=True)
+
+        pending = []
+
+        def extract(i):
+            first = i - (i % 2)
+            n = 2 * (i - first + 1)
+            t0 = 2 * first
+            if t0 % BATCH == 0:
+                state["raw"] = soft.tile([P, BATCH, 2, F], F32, name="raw", align_bytes=64)
+            raw, sb = state["raw"], state["s"]
+            o = t0 % BATCH
+            for b in range(B):
+                nc.scalar.copy(out=raw[32 * b : 32 * b + 32, o : o + n, :, :].rearrange("p j h g -> p j (h g)"), in_=sb[32 * b : 32 * b + 32, 0:n, 32 * b : 32 * b + 32])
+            if o + n == BATCH or t0 + n == HALF:
+                softmax(raw, o + n, t0 + n - (o + n))
+
+        def softmax(raw, n, t0):
+            odd = soft.tile([P, BATCH, F], F32, name="odd", align_bytes=64)
+            sel = soft.tile([P, BATCH, F], F32, name="sel", align_bytes=64)
+            mx = soft.tile([P, BATCH], F32, name="mx", align_bytes=64)
+            sub = soft.tile([P, BATCH, F], F32, name="sub", align_bytes=64)
+            ex = soft.tile([P, BATCH, F], F32, name="ex", align_bytes=64)
+            sm = soft.tile([P, BATCH], F32, name="sm", align_bytes=64)
+            rc = soft.tile([P, BATCH], F32, name="rc", align_bytes=64)
+            res = outs.tile([P, BATCH, F], F32, name="res", align_bytes=64)
+
+            def wide(v):
+                return v[:, 0:n].unsqueeze(2).to_broadcast([P, n, F])
+
+            def s1():
+                nc.vector.tensor_scalar(out=odd[:, 0:n, :], in0=raw[:, 0:n, 1, :], scalar1=pick[:, 1:2], scalar2=None, op0=ALU.mult)
+
+            def s2():
+                nc.vector.scalar_tensor_tensor(out=sel[:, 0:n, :], in0=raw[:, 0:n, 0, :], scalar=pick[:, 0:1], in1=odd[:, 0:n, :], op0=ALU.mult, op1=ALU.add)
+
+            def s3():
+                nc.vector.tensor_reduce(out=mx[:, 0:n], in_=sel[:, 0:n, :], axis=AX.X, op=ALU.max)
+
+            def s4():
+                nc.vector.tensor_tensor(out=sub[:, 0:n, :], in0=sel[:, 0:n, :], in1=wide(mx), op=ALU.subtract)
+                nc.scalar.activation(out=ex[:, 0:n, :], in_=sub[:, 0:n, :], func=ACT.Exp, scale=0.125)
+
+            def s5():
+                nc.vector.tensor_reduce(out=sm[:, 0:n], in_=ex[:, 0:n, :], axis=AX.X, op=ALU.add)
+
+            def s6():
+                nc.vector.reciprocal(out=rc[:, 0:n], in_=sm[:, 0:n])
+
+            def s7():
+                nc.vector.tensor_tensor(out=res[:, 0:n, :], in0=ex[:, 0:n, :], in1=wide(rc), op=ALU.mult)
+                for b in range(B):
+                    for h in range(2):
+                        nc.sync.dma_start(
+                            out=out[b, 0, h * HALF + t0 : h * HALF + t0 + n, :, :].rearrange("n f g -> f n g"),
+                            in_=res[32 * b + h : 32 * b + 32 : 2, 0:n, :],
+                        )
+
+            pending.extend([s1, s2, s3, s4, s5, s6, s7])
+
+        def weights():
+            nc.vector.tensor_copy(out=w_perm[:].rearrange("p (t m b) -> p t m b", t=4, b=2), in_=w_raw[:].rearrange("p (m t b) -> p t m b", t=4, b=2))
+            nc.vector.tensor_copy(out=ws_perm[:].rearrange("p (t m) -> p t m", t=4), in_=ws_raw[:].rearrange("p (m t) -> p t m", t=4))
+            nc.vector.tensor_copy(out=bqf[:], in_=bq_raw[:])
+            for h in range(2):
+                nc.vector.tensor_reduce(out=pick[:, h : h + 1], in_=ident[:, h:P:2], axis=AX.X, op=ALU.add)
+
+        def ok(i):
+            return 0 <= i < UNITS
+
+        scale_x_first()
+        for i in range(-2, UNITS + 3):
+            if ok(i):
+                project(i)
+                if not is_direct(i):
+                    bias_pairs(i)
+            if ok(i - 2):
+                scores(i - 2)
+                if i - 2 == UNITS - 1 or (i - 2) % 2 == 1:
+                    extract(i - 2)
+            if ok(i + 2):
+                transposes(i + 2)
+                copies(i + 2)
+            if ok(i + 3):
+                scale_x(i + 3)
+            if i == -2:
+                weights()
+            if ok(i - 1) and not is_direct(i - 1):
+                weave(i - 1)
+            if ok(i + 1):
+                quant_xk(i + 1)
+            if pending:
+                pending.pop(0)()
+            if ok(i - 1):
+                quant_q(i - 1)
+            if ok(i) and is_direct(i):
+                bias_direct(i)
+        while pending:
+            pending.pop(0)()

@@ -23,7 +23,7 @@ P = 128
 HALF = 98
 UNITS = HALF // 2
 X_CHUNKS = [2] + [8] * 12
-K_CHUNKS = [2, 4, 8] + [14] * 6
+CHUNKS = HALF // 8
 BATCH = 16
 
 
@@ -39,6 +39,7 @@ def tile_dividedspacetimeattention_pa_t_w4_kernel(tc, x_bytes, x_scale, Wq_words
         work = ctx.enter_context(tc.tile_pool(name="work", bufs=3))
         codes = ctx.enter_context(tc.tile_pool(name="codes", bufs=5))
         soft = ctx.enter_context(tc.tile_pool(name="soft", bufs=2))
+        kgs = ctx.enter_context(tc.tile_pool(name="kgs", bufs=2))
         outs = ctx.enter_context(tc.tile_pool(name="outs", bufs=4))
         ps_t = ctx.enter_context(tc.psum_pool(name="ps_t", bufs=2))
         ps_y = ctx.enter_context(tc.psum_pool(name="ps_y", bufs=3))
@@ -54,24 +55,27 @@ def tile_dividedspacetimeattention_pa_t_w4_kernel(tc, x_bytes, x_scale, Wq_words
         x_tiles = []
         for c, n in enumerate(X_CHUNKS):
             x_tiles.append(big.tile([P, n * D], U8, name=f"x8_{c}", align_bytes=64))
-        k_view = k.rearrange("b o (h j) g d -> (b o h) g j d", j=HALF)
+        k_rows = k.rearrange("b o (h n) g d -> (n g) (b o h) d", h=2)
         k_tiles = []
-        for c, n in enumerate(K_CHUNKS):
-            k_tiles.append(big.tile([P, n, D], BF16, name=f"kraw_{c}", align_bytes=64))
-        x_at, k_at = [], []
+        for m in range(CHUNKS):
+            k_tiles.append(big.tile([P, 8, D], BF16, name=f"kraw_{m}", align_bytes=64))
+        k_last = big.tile([P, 2, D], BF16, name="kraw_last", align_bytes=64)
+        x_at = []
         for c, n in enumerate(X_CHUNKS):
             x_at += [(c, o) for o in range(n)]
-        for c, n in enumerate(K_CHUNKS):
-            k_at += [(c, o) for o in range(n)]
 
         def load_x(c):
             o = sum(X_CHUNKS[:c]) * D
             nc.sync.dma_start(out=x_tiles[c][:], in_=x_rows[:, o : o + X_CHUNKS[c] * D])
 
-        def load_k(c):
-            o = sum(K_CHUNKS[:c])
-            for q in range(8):
-                nc.sync.dma_start(out=k_tiles[c][16 * q : 16 * q + 16, :, :], in_=k_view[q, :, o : o + K_CHUNKS[c], :])
+        def load_k(m, step):
+            for q in range(0, 8, step):
+                nc.sync.dma_start(out=k_tiles[m][:, q : q + step, :], in_=k_rows[P * m : P * m + P, q : q + step, :])
+
+        def load_k_last():
+            for c in range(8):
+                r = 32 * (c % 4)
+                nc.sync.dma_start(out=k_last[r : r + 32, c // 4, :], in_=k_rows[P * CHUNKS : P * CHUNKS + 32, c, :])
 
         scale = const.tile([P, 2 * D], F32, name="scale", align_bytes=64)
         bq_raw = const.tile([P, 4], BF16, name="bq_raw")
@@ -83,28 +87,25 @@ def tile_dividedspacetimeattention_pa_t_w4_kernel(tc, x_bytes, x_scale, Wq_words
 
         load_x(0)
         nc.sync.dma_start(out=scale[:, 0:D], in_=x_scale.rearrange("a b k -> (a b k)").partition_broadcast(P))
-        load_k(0)
+        load_k(0, 2)
         nc.sync.dma_start(out=w_raw[:], in_=Wq_words[0])
         for q in range(4):
             nc.sync.dma_start(out=ws_raw[32 * q : 32 * q + 4, :].bitcast(I32), in_=Wq_scales[0, 4 * q : 4 * q + 4, :].bitcast(I32))
         nc.sync.dma_start(out=bq_raw[:], in_=bq.rearrange("(p t) -> p t", t=4))
-        load_x(1)
-        load_k(1)
-        load_k(2)
-        load_x(2)
-        nx = 3
-        for c in range(3, len(K_CHUNKS)):
-            load_k(c)
-            for r in range(2):
-                if nx < len(X_CHUNKS):
-                    load_x(nx)
-                    nx += 1
+        for m in range(1, CHUNKS):
+            load_x(m)
+            load_k(m, 4)
+        load_x(CHUNKS)
+        load_k_last()
 
         warm = const.tile([P, 1], F32, name="warm")
         nc.scalar.activation(out=warm[:], in_=ident[:, 0:1], func=ACT.Exp)
+        perm = const.tile([P, P], F32, name="perm")
+        nc.scalar.copy(out=perm[:].rearrange("p (b h f) -> p b h f", b=4, h=2), in_=ident[:].rearrange("p (b f h) -> p b h f", b=4, h=2))
         nc.scalar.copy(out=scale[:, D : 2 * D], in_=scale[:, 0:D])
 
-        xb, xk_of, c_of, cs_of, yb_of, qp_of, qg_of, qc_of, qcs_of, t_of = {}, {}, {}, {}, {}, {}, {}, {}, {}, {}
+        xb, xk_of, c_of, cs_of, yb_of, qp_of, qg_of, qc_of, qcs_of, t_of, kc_of, kcs_of = {}, {}, {}, {}, {}, {}, {}, {}, {}, {}, {}, {}
+        state = {}
 
         def scale_x(i):
             t = work.tile([P, 2 * D], BF16, name="xb", align_bytes=64)
@@ -118,37 +119,64 @@ def tile_dividedspacetimeattention_pa_t_w4_kernel(tc, x_bytes, x_scale, Wq_words
                 nc.vector.tensor_tensor(out=t[:, a * D : (a + 1) * D], in0=x_tiles[0][:, a * D : (a + 1) * D].bitcast(FP8), in1=scale[:, 0:D], op=ALU.mult)
             xb[0] = t
 
-        def transposes(i):
-            tx = ps_t.tile([P, 2, 2, P], F32, name="tx")
-            tk = ps_t.tile([P, 2, 2, P], F32, name="tk")
+        def transpose_x(i):
+            tx = ps_t.tile([P, 2, 8, 2, F], F32, name="tx")
             words = xb.pop(i)[:].bitcast(F32)
             for a in range(2):
                 for u in range(2):
-                    nc.tensor.transpose(tx[:, a, u, :], words[:, 256 * a + u : 256 * (a + 1) : 2], ident[:])
-            for a in range(2):
-                c, o = k_at[2 * i + a]
-                kw = k_tiles[c][:, o, :].bitcast(F32)
-                for u in range(2):
-                    nc.tensor.transpose(tk[:, a, u, :], kw[:, u:256:2], ident[:])
-            t_of[i] = (tx, tk)
+                    nc.tensor.transpose(tx[:, u, :, a, :], words[:, 256 * a + u : 256 * (a + 1) : 2], perm[:])
+            t_of[i] = tx
 
-        def copies(i):
-            xk = work.tile([P, 2, 1024], BF16, name="xk", align_bytes=64)
-            for s, t in enumerate(t_of.pop(i)):
-                nc.scalar.copy(out=xk[:, s, :].bitcast(F32).rearrange("p (a r u) -> p a r u", a=2, u=2), in_=t[:].rearrange("p a u r -> p a r u"))
-            xk_of[i] = xk
+        def copy_x(i):
+            xg = work.tile([P, 1024], BF16, name="xg", align_bytes=64)
+            nc.scalar.copy(out=xg[:].bitcast(F32).rearrange("p (n u) -> p n u", u=2), in_=t_of.pop(i)[:].rearrange("p u c a f -> p (c a f) u"))
+            xk_of[i] = xg
 
-        def quant_xk(i):
-            c = codes.tile([P, 512], U32, name="xk_codes", align_bytes=64)
-            s = codes.tile([P, 512], U8, name="xk_scales", align_bytes=64)
-            nc.vector.quantize_mx(out=c[:].bitcast(FP8X4), scales=s[:], in_=xk_of.pop(i)[:].rearrange("p s n -> p (s n)"))
+        def transpose_k(j):
+            m, q = divmod(j, 4)
+            if m < CHUNKS:
+                tk = ps_t.tile([P, 2, 4, 2, 32], F32, name="tk")
+                for e in range(2):
+                    kw = k_tiles[m][:, 2 * q + e, :].bitcast(F32)
+                    for u in range(2):
+                        nc.tensor.transpose(tk[:, u, :, e, :], kw[:, u:256:2], ident[:])
+            else:
+                tk = ps_t.tile([P, 2, 2, P], F32, name="tk")
+                for a in range(2):
+                    kw = k_last[:, a, :].bitcast(F32)
+                    for u in range(2):
+                        nc.tensor.transpose(tk[:, u, a, :], kw[:, u:256:2], ident[:])
+            state["tk"] = tk
+
+        def copy_k(j):
+            m, q = divmod(j, 4)
+            tk = state["tk"]
+            if q == 0:
+                state["kg", m] = kgs.tile([P, 4, 1024], BF16, name="kg", align_bytes=64)
+            kg = state["kg", m]
+            if m < CHUNKS:
+                kw = kg[:].rearrange("p a n -> p (a n)").bitcast(F32).rearrange("p (a n u) -> p a n u", a=4, u=2)
+                nc.scalar.copy(out=kw[:, :, 64 * q : 64 * q + 64, :], in_=tk[:].rearrange("p u a e r -> p a (e r) u"))
+            else:
+                nc.scalar.copy(out=kg[:, 0, :].bitcast(F32).rearrange("p (n u) -> p n u", u=2), in_=tk[:].rearrange("p u a r -> p (a r) u"))
+
+        def quant_x(i):
+            c = codes.tile([P, 256], U32, name="x_codes", align_bytes=64)
+            s = codes.tile([P, 256], U8, name="x_scales", align_bytes=64)
+            nc.vector.quantize_mx(out=c[:].bitcast(FP8X4), scales=s[:], in_=xk_of.pop(i)[:])
             c_of[i], cs_of[i] = c, s
+
+        def quant_k(i):
+            c = codes.tile([P, 256], U32, name="k_codes", align_bytes=64)
+            s = codes.tile([P, 256], U8, name="k_scales", align_bytes=64)
+            nc.vector.quantize_mx(out=c[:].bitcast(FP8X4), scales=s[:], in_=state["kg", i // 4][:, i % 4, :])
+            kc_of[i], kcs_of[i] = c, s
 
         def w_cols(t):
             return dict(lhsT=w_perm[:, 256 * t : 256 * t + 256].bitcast(FP4X4), lhsT_scale=ws_perm[:, 128 * t : 128 * t + 128])
 
         def project(i):
-            c, s = c_of[i], cs_of[i]
+            c, s = c_of.pop(i), cs_of.pop(i)
             banks = []
             for h in range(2):
                 if is_direct(i):
@@ -190,17 +218,14 @@ def tile_dividedspacetimeattention_pa_t_w4_kernel(tc, x_bytes, x_scale, Wq_words
             nc.vector.quantize_mx(out=c[:].bitcast(FP8X4), scales=s[:], in_=qg_of.pop(i)[:].rearrange("p n t -> p (n t)"))
             qc_of[i], qcs_of[i] = c, s
 
-        state = {}
-
         def scores(i):
             if i % 2 == 0:
                 state["s"] = ps_s.tile([P, 4, P], F32, name="sb")
             sb = state["s"]
-            qc, qs, kc, ks = qc_of.pop(i), qcs_of.pop(i), c_of.pop(i), cs_of.pop(i)
+            qc, qs, kc, ks = qc_of.pop(i), qcs_of.pop(i), kc_of.pop(i), kcs_of.pop(i)
             for a in range(2):
                 q_cols = slice(P * a, P * a + P)
-                k_cols = slice(256 + P * a, 256 + P * a + P)
-                nc.tensor.matmul_mx(out=sb[:, 2 * (i % 2) + a, :], lhsT=qc[:, q_cols].bitcast(FP8X4), lhsT_scale=qs[:, q_cols], rhs=kc[:, k_cols].bitcast(FP8X4), rhs_scale=ks[:, k_cols], start=True, stop=True)
+                nc.tensor.matmul_mx(out=sb[:, 2 * (i % 2) + a, :], lhsT=qc[:, q_cols].bitcast(FP8X4), lhsT_scale=qs[:, q_cols], rhs=kc[:, q_cols].bitcast(FP8X4), rhs_scale=ks[:, q_cols], start=True, stop=True)
 
         pending = []
 
@@ -251,12 +276,13 @@ def tile_dividedspacetimeattention_pa_t_w4_kernel(tc, x_bytes, x_scale, Wq_words
 
             def s7():
                 nc.vector.tensor_tensor(out=res[:, 0:n, :], in0=ex[:, 0:n, :], in1=wide(rc), op=ALU.mult)
-                for b in range(B):
-                    for h in range(2):
-                        nc.sync.dma_start(
-                            out=out[b, 0, h * HALF + t0 : h * HALF + t0 + n, :, :].rearrange("n f g -> f n g"),
-                            in_=res[32 * b + h : 32 * b + 32 : 2, 0:n, :],
-                        )
+                for c in range(8):
+                    first = (c % 2) * HALF + t0
+                    r = 32 * (c % 4)
+                    nc.sync.dma_start(
+                        out=out[c // 2, 0, first : first + n, :, :].rearrange("(u s) f g -> (s f) u g", s=2),
+                        in_=res[r : r + 32, c // 4 : n : 2, :],
+                    )
 
             pending.extend([s1, s2, s3, s4, s5, s6, s7])
 
@@ -265,13 +291,13 @@ def tile_dividedspacetimeattention_pa_t_w4_kernel(tc, x_bytes, x_scale, Wq_words
             nc.vector.tensor_copy(out=ws_perm[:].rearrange("p (t m) -> p t m", t=4), in_=ws_raw[:].rearrange("p (m t) -> p t m", t=4))
             nc.vector.tensor_copy(out=bqf[:], in_=bq_raw[:])
             for h in range(2):
-                nc.vector.tensor_reduce(out=pick[:, h : h + 1], in_=ident[:, h:P:2], axis=AX.X, op=ALU.add)
+                nc.vector.tensor_reduce(out=pick[:, h : h + 1], in_=ident[:].rearrange("p (a s f) -> p s a f", s=2, f=F)[:, h, :, :], axis=AX.XY, op=ALU.add)
 
         def ok(i):
             return 0 <= i < UNITS
 
         scale_x_first()
-        for i in range(-2, UNITS + 3):
+        for i in range(-3, UNITS + 3):
             if ok(i):
                 project(i)
                 if not is_direct(i):
@@ -280,20 +306,24 @@ def tile_dividedspacetimeattention_pa_t_w4_kernel(tc, x_bytes, x_scale, Wq_words
                 scores(i - 2)
                 if i - 2 == UNITS - 1 or (i - 2) % 2 == 1:
                     extract(i - 2)
-            if ok(i + 2):
-                transposes(i + 2)
-                copies(i + 2)
             if ok(i + 3):
+                transpose_k(i + 3)
+                copy_k(i + 3)
+            if ok(i + 2):
+                transpose_x(i + 2)
+                copy_x(i + 2)
+            if i > -3 and ok(i + 3):
                 scale_x(i + 3)
             if i == -2:
                 weights()
             if ok(i - 1) and not is_direct(i - 1):
                 weave(i - 1)
             if ok(i + 1):
-                quant_xk(i + 1)
+                quant_x(i + 1)
             if pending:
                 pending.pop(0)()
             if ok(i - 1):
+                quant_k(i - 1)
                 quant_q(i - 1)
             if ok(i) and is_direct(i):
                 bias_direct(i)

@@ -181,11 +181,11 @@ def tile_dividedspacetimeattention_pa_t_w4_kernel(tc, x_bytes, x_scale, Wq_words
             for h in range(2):
                 if is_direct(i):
                     yb = ps_y.tile([P, 4, P], F32, name="yb")
-                    for t in range(4):
+                    for t in [0, 1, 2, 3] * 2:
                         nc.tensor.matmul_mx(out=yb[:, t, :], rhs=c[:, P * h : P * h + P].bitcast(FP8X4), rhs_scale=s[:, P * h : P * h + P], start=True, stop=True, **w_cols(t))
                 else:
                     yb = ps_y.tile([P, 2, 2 * P], F32, name="yb")
-                    for e in range(2):
+                    for e in [0, 1] * 2:
                         nc.tensor.matmul_mx(out=yb[:, e, :], rhs=c[:, 0:256].bitcast(FP8X4), rhs_scale=s[:, 0:256], start=True, stop=True, **w_cols(2 * h + e))
                 banks.append(yb)
             yb_of[i] = banks

@@ -27,8 +27,7 @@ CHUNKS = HALF // 8
 BATCH = 16
 
 
-def is_direct(i):
-    return i % 4 == 3
+REPEAT = 4
 
 
 def tile_dividedspacetimeattention_pa_t_w4_kernel(tc, x_bytes, x_scale, Wq_words, Wq_scales, bq, k, out):
@@ -37,7 +36,8 @@ def tile_dividedspacetimeattention_pa_t_w4_kernel(tc, x_bytes, x_scale, Wq_words
         const = ctx.enter_context(tc.tile_pool(name="const", bufs=1))
         big = ctx.enter_context(tc.tile_pool(name="big", bufs=1))
         work = ctx.enter_context(tc.tile_pool(name="work", bufs=3))
-        codes = ctx.enter_context(tc.tile_pool(name="codes", bufs=5))
+        xqs = ctx.enter_context(tc.tile_pool(name="xqs", bufs=4))
+        codes = ctx.enter_context(tc.tile_pool(name="codes", bufs=4))
         soft = ctx.enter_context(tc.tile_pool(name="soft", bufs=2))
         kgs = ctx.enter_context(tc.tile_pool(name="kgs", bufs=2))
         outs = ctx.enter_context(tc.tile_pool(name="outs", bufs=4))
@@ -104,8 +104,11 @@ def tile_dividedspacetimeattention_pa_t_w4_kernel(tc, x_bytes, x_scale, Wq_words
         nc.scalar.copy(out=perm[:].rearrange("p (b h f) -> p b h f", b=4, h=2), in_=ident[:].rearrange("p (b f h) -> p b h f", b=4, h=2))
         nc.scalar.copy(out=scale[:, D : 2 * D], in_=scale[:, 0:D])
 
-        xb, xk_of, c_of, cs_of, yb_of, qp_of, qg_of, qc_of, qcs_of, t_of, kc_of, kcs_of = {}, {}, {}, {}, {}, {}, {}, {}, {}, {}, {}, {}
+        xb, xg_of, xq_of, yb_of, qp_of, t_of, kc_of = {}, {}, {}, {}, {}, {}, {}
         state = {}
+
+        def ok(i):
+            return 0 <= i < UNITS
 
         def scale_x(i):
             t = work.tile([P, 2 * D], BF16, name="xb", align_bytes=64)
@@ -128,9 +131,7 @@ def tile_dividedspacetimeattention_pa_t_w4_kernel(tc, x_bytes, x_scale, Wq_words
             t_of[i] = tx
 
         def copy_x(i):
-            xg = work.tile([P, 1024], BF16, name="xg", align_bytes=64)
-            nc.scalar.copy(out=xg[:].bitcast(F32).rearrange("p (n u) -> p n u", u=2), in_=t_of.pop(i)[:].rearrange("p u c a f -> p (c a f) u"))
-            xk_of[i] = xg
+            nc.scalar.copy(out=xg_of[i][:, 0, :].bitcast(F32).rearrange("p (n u) -> p n u", u=2), in_=t_of.pop(i)[:].rearrange("p u c a f -> p (c a f) u"))
 
         def transpose_k(j):
             m, q = divmod(j, 4)
@@ -160,72 +161,63 @@ def tile_dividedspacetimeattention_pa_t_w4_kernel(tc, x_bytes, x_scale, Wq_words
             else:
                 nc.scalar.copy(out=kg[:, 0, :].bitcast(F32).rearrange("p (n u) -> p n u", u=2), in_=tk[:].rearrange("p u a r -> p (a r) u"))
 
-        def quant_x(i):
-            c = codes.tile([P, 256], U32, name="x_codes", align_bytes=64)
-            s = codes.tile([P, 256], U8, name="x_scales", align_bytes=64)
-            nc.vector.quantize_mx(out=c[:].bitcast(FP8X4), scales=s[:], in_=xk_of.pop(i)[:])
-            c_of[i], cs_of[i] = c, s
-
-        def quant_k(i):
-            c = codes.tile([P, 256], U32, name="k_codes", align_bytes=64)
-            s = codes.tile([P, 256], U8, name="k_scales", align_bytes=64)
-            nc.vector.quantize_mx(out=c[:].bitcast(FP8X4), scales=s[:], in_=state["kg", i // 4][:, i % 4, :])
-            kc_of[i], kcs_of[i] = c, s
+        def quant_k(p):
+            n = 2 if ok(2 * p + 1) else 1
+            c = codes.tile([P, 512], U32, name="k_codes", align_bytes=64)
+            s = codes.tile([P, 512], U8, name="k_scales", align_bytes=64)
+            o = (2 * p) % 4
+            nc.vector.quantize_mx(out=c[:, 0 : 256 * n].bitcast(FP8X4), scales=s[:, 0 : 256 * n], in_=state["kg", p // 2][:, o : o + n, :].rearrange("p a n -> p (a n)"))
+            kc_of[p] = (c, s)
 
         def w_cols(t):
             return dict(lhsT=w_perm[:, 256 * t : 256 * t + 256].bitcast(FP4X4), lhsT_scale=ws_perm[:, 128 * t : 128 * t + 128])
 
         def project(i):
-            c, s = c_of.pop(i), cs_of.pop(i)
+            c, s = xq_of[i]
             banks = []
             for h in range(2):
-                if is_direct(i):
-                    yb = ps_y.tile([P, 4, P], F32, name="yb")
-                    for t in [0, 1, 2, 3] * 2:
-                        nc.tensor.matmul_mx(out=yb[:, t, :], rhs=c[:, P * h : P * h + P].bitcast(FP8X4), rhs_scale=s[:, P * h : P * h + P], start=True, stop=True, **w_cols(t))
-                else:
-                    yb = ps_y.tile([P, 2, 2 * P], F32, name="yb")
-                    for e in [0, 1] * 2:
-                        nc.tensor.matmul_mx(out=yb[:, e, :], rhs=c[:, 0:256].bitcast(FP8X4), rhs_scale=s[:, 0:256], start=True, stop=True, **w_cols(2 * h + e))
+                yb = ps_y.tile([P, 2, 2 * P], F32, name="yb")
+                for e in range(2):
+                    nc.tensor.matmul_mx(out=yb[:, e, :], rhs=c[:, 0:256].bitcast(FP8X4), rhs_scale=s[:, 0:256], start=True, stop=True, **w_cols(2 * h + e))
                 banks.append(yb)
             yb_of[i] = banks
 
-        def bias_pairs(i):
-            qp = work.tile([P, 2, 256, 2], BF16, name="qp", align_bytes=64)
-            for u, yb in enumerate(yb_of.pop(i)):
+        def add_bias(i):
+            qp = work.tile([P, 4, 256], BF16, name="qp", align_bytes=64)
+            for h, yb in enumerate(yb_of.pop(i)):
                 for e in range(2):
-                    t = 2 * u + e
-                    nc.scalar.activation(out=qp[:, u, :, e], in_=yb[:, e, :], func=ACT.Identity, bias=bqf[:, t : t + 1], scale=1.0)
+                    t = 2 * h + e
+                    nc.scalar.activation(out=qp[:, t, :], in_=yb[:, e, :], func=ACT.Identity, bias=bqf[:, t : t + 1], scale=1.0)
             qp_of[i] = qp
 
+        def new_xq(i):
+            xg_of[i] = xqs.tile([P, 2, 1024], BF16, name="xq", align_bytes=64)
+
         def weave(i):
-            qg = work.tile([P, 256, 4], BF16, name="qg", align_bytes=64)
             nc.vector.tensor_copy(
-                out=qg[:].rearrange("p n t -> p (n t)").bitcast(F32).rearrange("p (n u) -> p n u", u=2),
-                in_=qp_of.pop(i)[:].rearrange("p u n e -> p (u n e)").bitcast(F32).rearrange("p (u n) -> p n u", u=2),
+                out=xg_of[i + 2][:, 1, :].rearrange("p (c i t) -> p c t i", i=4, t=4),
+                in_=qp_of.pop(i)[:].rearrange("p t (c i) -> p c t i", i=4),
             )
-            qg_of[i] = qg
 
-        def bias_direct(i):
-            qg = work.tile([P, 256, 4], BF16, name="qg", align_bytes=64)
-            for h, yb in enumerate(yb_of.pop(i)):
-                nc.vector.tensor_tensor(out=qg[:, P * h : P * h + P, :], in0=yb[:].rearrange("p t n -> p n t"), in1=bqf[:].unsqueeze(1).to_broadcast([P, P, 4]), op=ALU.add)
-            qg_of[i] = qg
-
-        def quant_q(i):
-            c = codes.tile([P, 256], U32, name="q_codes", align_bytes=64)
-            s = codes.tile([P, 256], U8, name="q_scales", align_bytes=64)
-            nc.vector.quantize_mx(out=c[:].bitcast(FP8X4), scales=s[:], in_=qg_of.pop(i)[:].rearrange("p n t -> p (n t)"))
-            qc_of[i], qcs_of[i] = c, s
+        def quant_xq(i):
+            xq = xg_of.pop(i)
+            c = codes.tile([P, 512], U32, name="xq_codes", align_bytes=64)
+            s = codes.tile([P, 512], U8, name="xq_scales", align_bytes=64)
+            lo, hi = (0 if ok(i) else 1), (2 if ok(i - 2) else 1)
+            nc.vector.quantize_mx(out=c[:, 256 * lo : 256 * hi].bitcast(FP8X4), scales=s[:, 256 * lo : 256 * hi], in_=xq[:, lo:hi, :].rearrange("p s n -> p (s n)"))
+            xq_of[i] = (c, s)
 
         def scores(i):
             if i % 2 == 0:
                 state["s"] = ps_s.tile([P, 4, P], F32, name="sb")
             sb = state["s"]
-            qc, qs, kc, ks = qc_of.pop(i), qcs_of.pop(i), kc_of.pop(i), kcs_of.pop(i)
+            qc, qs = xq_of.pop(i + 2)
+            kc, ks = kc_of[i // 2]
             for a in range(2):
-                q_cols = slice(P * a, P * a + P)
-                nc.tensor.matmul_mx(out=sb[:, 2 * (i % 2) + a, :], lhsT=qc[:, q_cols].bitcast(FP8X4), lhsT_scale=qs[:, q_cols], rhs=kc[:, q_cols].bitcast(FP8X4), rhs_scale=ks[:, q_cols], start=True, stop=True)
+                q_cols = slice(256 + P * a, 256 + P * a + P)
+                k_cols = slice(256 * (i % 2) + P * a, 256 * (i % 2) + P * a + P)
+                for r in range(REPEAT):
+                    nc.tensor.matmul_mx(out=sb[:, 2 * (i % 2) + a, :], lhsT=qc[:, q_cols].bitcast(FP8X4), lhsT_scale=qs[:, q_cols], rhs=kc[:, k_cols].bitcast(FP8X4), rhs_scale=ks[:, k_cols], start=True, stop=True)
 
         pending = []
 
@@ -293,39 +285,37 @@ def tile_dividedspacetimeattention_pa_t_w4_kernel(tc, x_bytes, x_scale, Wq_words
             for h in range(2):
                 nc.vector.tensor_reduce(out=pick[:, h : h + 1], in_=ident[:].rearrange("p (a s f) -> p s a f", s=2, f=F)[:, h, :, :], axis=AX.XY, op=ALU.add)
 
-        def ok(i):
-            return 0 <= i < UNITS
-
         scale_x_first()
         for i in range(-3, UNITS + 3):
             if ok(i):
                 project(i)
-                if not is_direct(i):
-                    bias_pairs(i)
+                add_bias(i)
+            if ok(i + 3):
+                transpose_k(i + 3)
+                copy_k(i + 3)
             if ok(i - 2):
                 scores(i - 2)
                 if i - 2 == UNITS - 1 or (i - 2) % 2 == 1:
                     extract(i - 2)
-            if ok(i + 3):
-                transpose_k(i + 3)
-                copy_k(i + 3)
+            if ok(i + 2) or ok(i):
+                new_xq(i + 2)
             if ok(i + 2):
                 transpose_x(i + 2)
                 copy_x(i + 2)
+            if ok(i - 1):
+                weave(i - 1)
+            if i % 2 == 0 and pending:
+                pending.pop(0)()
             if i > -3 and ok(i + 3):
                 scale_x(i + 3)
             if i == -2:
                 weights()
-            if ok(i - 1) and not is_direct(i - 1):
-                weave(i - 1)
-            if ok(i + 1):
-                quant_x(i + 1)
-            if pending:
-                pending.pop(0)()
-            if ok(i - 1):
-                quant_k(i - 1)
-                quant_q(i - 1)
-            if ok(i) and is_direct(i):
-                bias_direct(i)
+            if ok(i + 1) or ok(i - 1):
+                quant_xq(i + 1)
+            if i % 2 == 0:
+                if pending:
+                    pending.pop(0)()
+            elif ok(i - 1):
+                quant_k((i - 1) // 2)
         while pending:
             pending.pop(0)()

from contextlib import ExitStack

import concourse.mybir as mybir
from concourse.masks import make_identity

B, N, F, D = 4, 196, 16, 512
ROWS = B * N * F
FLOPS = 2 * ROWS * D * D + 2 * ROWS * F * D

F32 = mybir.dt.float32
BF16 = mybir.dt.bfloat16
I32 = mybir.dt.int32
U32 = mybir.dt.uint32
U8 = mybir.dt.uint8
FP8 = mybir.dt.float8_e4m3fn
FP8X4 = mybir.dt.float8_e4m3fn_x4
FP4X4 = mybir.dt.float4_e2m1fn_x4
ACT = mybir.ActivationFunctionType
ALU = mybir.AluOpType
AX = mybir.AxisListType

P = 128
HALF = 98
UNITS = HALF // 2
X_CHUNKS = [2] + [8] * 12
CHUNKS = HALF // 8
BATCH = 16


REPEAT = 4


def tile_dividedspacetimeattention_pa_t_w4_kernel(tc, x_bytes, x_scale, Wq_words, Wq_scales, bq, k, out):
    nc = tc.nc
    with ExitStack() as ctx:
        const = ctx.enter_context(tc.tile_pool(name="const", bufs=1))
        big = ctx.enter_context(tc.tile_pool(name="big", bufs=1))
        work = ctx.enter_context(tc.tile_pool(name="work", bufs=3))
        xqs = ctx.enter_context(tc.tile_pool(name="xqs", bufs=4))
        codes = ctx.enter_context(tc.tile_pool(name="codes", bufs=4))
        soft = ctx.enter_context(tc.tile_pool(name="soft", bufs=2))
        kgs = ctx.enter_context(tc.tile_pool(name="kgs", bufs=2))
        outs = ctx.enter_context(tc.tile_pool(name="outs", bufs=4))
        ps_t = ctx.enter_context(tc.psum_pool(name="ps_t", bufs=2))
        ps_y = ctx.enter_context(tc.psum_pool(name="ps_y", bufs=3))
        ps_s = ctx.enter_context(tc.psum_pool(name="ps_s", bufs=1))
        ctx.enter_context(tc.manual_schedule())

        ident = const.tile([P, P], F32, name="ident")
        make_identity(nc, ident[:])
        ws_raw = const.tile([P, D], U8, name="ws_raw", align_bytes=64)
        nc.gpsimd.memset(ws_raw[:].bitcast(I32), 0)

        x_rows = x_bytes.rearrange("b (q j) d -> (b q) (j d)", j=HALF)
        x_tiles = []
        for c, n in enumerate(X_CHUNKS):
            x_tiles.append(big.tile([P, n * D], U8, name=f"x8_{c}", align_bytes=64))
        k_rows = k.rearrange("b o (h n) g d -> (n g) (b o h) d", h=2)
        k_tiles = []
        for m in range(CHUNKS):
            k_tiles.append(big.tile([P, 8, D], BF16, name=f"kraw_{m}", align_bytes=64))
        k_last = big.tile([P, 2, D], BF16, name="kraw_last", align_bytes=64)
        x_at = []
        for c, n in enumerate(X_CHUNKS):
            x_at += [(c, o) for o in range(n)]

        def load_x(c):
            o = sum(X_CHUNKS[:c]) * D
            nc.sync.dma_start(out=x_tiles[c][:], in_=x_rows[:, o : o + X_CHUNKS[c] * D])

        def load_k(m, step):
            for q in range(0, 8, step):
                nc.sync.dma_start(out=k_tiles[m][:, q : q + step, :], in_=k_rows[P * m : P * m + P, q : q + step, :])

        def load_k_last():
            for c in range(8):
                r = 32 * (c % 4)
                nc.sync.dma_start(out=k_last[r : r + 32, c // 4, :], in_=k_rows[P * CHUNKS : P * CHUNKS + 32, c, :])

        scale = const.tile([P, 2 * D], F32, name="scale", align_bytes=64)
        bq_raw = const.tile([P, 4], BF16, name="bq_raw")
        w_raw = const.tile([P, 2 * D], U8, name="w_raw", align_bytes=64)
        w_perm = const.tile([P, 2 * D], U8, name="w_perm", align_bytes=64)
        ws_perm = const.tile([P, D], U8, name="ws_perm", align_bytes=64)
        bqf = const.tile([P, 4], F32, name="bqf")
        pick = const.tile([P, 2], F32, name="pick")

        load_x(0)
        nc.sync.dma_start(out=scale[:, 0:D], in_=x_scale.rearrange("a b k -> (a b k)").partition_broadcast(P))
        load_k(0, 2)
        nc.sync.dma_start(out=w_raw[:], in_=Wq_words[0])
        for q in range(4):
            nc.sync.dma_start(out=ws_raw[32 * q : 32 * q + 4, :].bitcast(I32), in_=Wq_scales[0, 4 * q : 4 * q + 4, :].bitcast(I32))
        nc.sync.dma_start(out=bq_raw[:], in_=bq.rearrange("(p t) -> p t", t=4))
        for m in range(1, CHUNKS):
            load_x(m)
            load_k(m, 4)
        load_x(CHUNKS)
        load_k_last()

        warm = const.tile([P, 1], F32, name="warm")
        nc.scalar.activation(out=warm[:], in_=ident[:, 0:1], func=ACT.Exp)
        perm = const.tile([P, P], F32, name="perm")
        nc.scalar.copy(out=perm[:].rearrange("p (b h f) -> p b h f", b=4, h=2), in_=ident[:].rearrange("p (b f h) -> p b h f", b=4, h=2))
        nc.scalar.copy(out=scale[:, D : 2 * D], in_=scale[:, 0:D])

        xb, xg_of, xq_of, yb_of, qp_of, t_of, kc_of = {}, {}, {}, {}, {}, {}, {}
        state = {}

        def ok(i):
            return 0 <= i < UNITS

        def scale_x(i):
            t = work.tile([P, 2 * D], BF16, name="xb", align_bytes=64)
            c, o = x_at[2 * i]
            nc.vector.tensor_tensor(out=t[:], in0=x_tiles[c][:, o * D : (o + 2) * D].bitcast(FP8), in1=scale[:], op=ALU.mult)
            xb[i] = t

        def scale_x_first():
            t = work.tile([P, 2 * D], BF16, name="xb", align_bytes=64)
            for a in range(2):
                nc.vector.tensor_tensor(out=t[:, a * D : (a + 1) * D], in0=x_tiles[0][:, a * D : (a + 1) * D].bitcast(FP8), in1=scale[:, 0:D], op=ALU.mult)
            xb[0] = t

        def transpose_x(i):
            tx = ps_t.tile([P, 2, 8, 2, F], F32, name="tx")
            words = xb.pop(i)[:].bitcast(F32)
            for a in range(2):
                for u in range(2):
                    nc.tensor.transpose(tx[:, u, :, a, :], words[:, 256 * a + u : 256 * (a + 1) : 2], perm[:])
            t_of[i] = tx

        def copy_x(i):
            nc.scalar.copy(out=xg_of[i][:, 0, :].bitcast(F32).rearrange("p (n u) -> p n u", u=2), in_=t_of.pop(i)[:].rearrange("p u c a f -> p (c a f) u"))

        def transpose_k(j):
            m, q = divmod(j, 4)
            if m < CHUNKS:
                tk = ps_t.tile([P, 2, 4, 2, 32], F32, name="tk")
                for e in range(2):
                    kw = k_tiles[m][:, 2 * q + e, :].bitcast(F32)
                    for u in range(2):
                        nc.tensor.transpose(tk[:, u, :, e, :], kw[:, u:256:2], ident[:])
            else:
                tk = ps_t.tile([P, 2, 2, P], F32, name="tk")
                for a in range(2):
                    kw = k_last[:, a, :].bitcast(F32)
                    for u in range(2):
                        nc.tensor.transpose(tk[:, u, a, :], kw[:, u:256:2], ident[:])
            state["tk"] = tk

        def copy_k(j):
            m, q = divmod(j, 4)
            tk = state["tk"]
            if q == 0:
                state["kg", m] = kgs.tile([P, 4, 1024], BF16, name="kg", align_bytes=64)
            kg = state["kg", m]
            if m < CHUNKS:
                kw = kg[:].rearrange("p a n -> p (a n)").bitcast(F32).rearrange("p (a n u) -> p a n u", a=4, u=2)
                nc.scalar.copy(out=kw[:, :, 64 * q : 64 * q + 64, :], in_=tk[:].rearrange("p u a e r -> p a (e r) u"))
            else:
                nc.scalar.copy(out=kg[:, 0, :].bitcast(F32).rearrange("p (n u) -> p n u", u=2), in_=tk[:].rearrange("p u a r -> p (a r) u"))

        def quant_k(p):
            n = 2 if ok(2 * p + 1) else 1
            c = codes.tile([P, 512], U32, name="k_codes", align_bytes=64)
            s = codes.tile([P, 512], U8, name="k_scales", align_bytes=64)
            o = (2 * p) % 4
            nc.vector.quantize_mx(out=c[:, 0 : 256 * n].bitcast(FP8X4), scales=s[:, 0 : 256 * n], in_=state["kg", p // 2][:, o : o + n, :].rearrange("p a n -> p (a n)"))
            kc_of[p] = (c, s)

        def w_cols(t):
            return dict(lhsT=w_perm[:, 256 * t : 256 * t + 256].bitcast(FP4X4), lhsT_scale=ws_perm[:, 128 * t : 128 * t + 128])

        def project(i):
            c, s = xq_of[i]
            banks = []
            for h in range(2):
                yb = ps_y.tile([P, 2, 2 * P], F32, name="yb")
                for e in range(2):
                    nc.tensor.matmul_mx(out=yb[:, e, :], rhs=c[:, 0:256].bitcast(FP8X4), rhs_scale=s[:, 0:256], start=True, stop=True, **w_cols(2 * h + e))
                banks.append(yb)
            yb_of[i] = banks

        def add_bias(i):
            qp = work.tile([P, 4, 256], BF16, name="qp", align_bytes=64)
            for h, yb in enumerate(yb_of.pop(i)):
                for e in range(2):
                    t = 2 * h + e
                    nc.scalar.activation(out=qp[:, t, :], in_=yb[:, e, :], func=ACT.Identity, bias=bqf[:, t : t + 1], scale=1.0)
            qp_of[i] = qp

        def new_xq(i):
            xg_of[i] = xqs.tile([P, 2, 1024], BF16, name="xq", align_bytes=64)

        def weave(i):
            nc.vector.tensor_copy(
                out=xg_of[i + 2][:, 1, :].rearrange("p (c i t) -> p c t i", i=4, t=4),
                in_=qp_of.pop(i)[:].rearrange("p t (c i) -> p c t i", i=4),
            )

        def quant_xq(i):
            xq = xg_of.pop(i)
            c = codes.tile([P, 512], U32, name="xq_codes", align_bytes=64)
            s = codes.tile([P, 512], U8, name="xq_scales", align_bytes=64)
            lo, hi = (0 if ok(i) else 1), (2 if ok(i - 2) else 1)
            nc.vector.quantize_mx(out=c[:, 256 * lo : 256 * hi].bitcast(FP8X4), scales=s[:, 256 * lo : 256 * hi], in_=xq[:, lo:hi, :].rearrange("p s n -> p (s n)"))
            xq_of[i] = (c, s)

        def scores(i):
            if i % 2 == 0:
                state["s"] = ps_s.tile([P, 4, P], F32, name="sb")
            sb = state["s"]
            qc, qs = xq_of.pop(i + 2)
            kc, ks = kc_of[i // 2]
            for a in range(2):
                q_cols = slice(256 + P * a, 256 + P * a + P)
                k_cols = slice(256 * (i % 2) + P * a, 256 * (i % 2) + P * a + P)
                for r in range(REPEAT):
                    nc.tensor.matmul_mx(out=sb[:, 2 * (i % 2) + a, :], lhsT=qc[:, q_cols].bitcast(FP8X4), lhsT_scale=qs[:, q_cols], rhs=kc[:, k_cols].bitcast(FP8X4), rhs_scale=ks[:, k_cols], start=True, stop=True)

        pending = []

        def extract(i):
            first = i - (i % 2)
            n = 2 * (i - first + 1)
            t0 = 2 * first
            if t0 % BATCH == 0:
                state["raw"] = soft.tile([P, BATCH, 2, F], F32, name="raw", align_bytes=64)
            raw, sb = state["raw"], state["s"]
            o = t0 % BATCH
            for b in range(B):
                nc.scalar.copy(out=raw[32 * b : 32 * b + 32, o : o + n, :, :].rearrange("p j h g -> p j (h g)"), in_=sb[32 * b : 32 * b + 32, 0:n, 32 * b : 32 * b + 32])
            if o + n == BATCH or t0 + n == HALF:
                softmax(raw, o + n, t0 + n - (o + n))

        def softmax(raw, n, t0):
            odd = soft.tile([P, BATCH, F], F32, name="odd", align_bytes=64)
            sel = soft.tile([P, BATCH, F], F32, name="sel", align_bytes=64)
            mx = soft.tile([P, BATCH], F32, name="mx", align_bytes=64)
            sub = soft.tile([P, BATCH, F], F32, name="sub", align_bytes=64)
            ex = soft.tile([P, BATCH, F], F32, name="ex", align_bytes=64)
            sm = soft.tile([P, BATCH], F32, name="sm", align_bytes=64)
            rc = soft.tile([P, BATCH], F32, name="rc", align_bytes=64)
            res = outs.tile([P, BATCH, F], F32, name="res", align_bytes=64)

            def wide(v):
                return v[:, 0:n].unsqueeze(2).to_broadcast([P, n, F])

            def s1():
                nc.vector.tensor_scalar(out=odd[:, 0:n, :], in0=raw[:, 0:n, 1, :], scalar1=pick[:, 1:2], scalar2=None, op0=ALU.mult)

            def s2():
                nc.vector.scalar_tensor_tensor(out=sel[:, 0:n, :], in0=raw[:, 0:n, 0, :], scalar=pick[:, 0:1], in1=odd[:, 0:n, :], op0=ALU.mult, op1=ALU.add)

            def s3():
                nc.vector.tensor_reduce(out=mx[:, 0:n], in_=sel[:, 0:n, :], axis=AX.X, op=ALU.max)

            def s4():
                nc.vector.tensor_tensor(out=sub[:, 0:n, :], in0=sel[:, 0:n, :], in1=wide(mx), op=ALU.subtract)
                nc.scalar.activation(out=ex[:, 0:n, :], in_=sub[:, 0:n, :], func=ACT.Exp, scale=0.125)

            def s5():
                nc.vector.tensor_reduce(out=sm[:, 0:n], in_=ex[:, 0:n, :], axis=AX.X, op=ALU.add)

            def s6():
                nc.vector.reciprocal(out=rc[:, 0:n], in_=sm[:, 0:n])

            def s7():
                nc.vector.tensor_tensor(out=res[:, 0:n, :], in0=ex[:, 0:n, :], in1=wide(rc), op=ALU.mult)
                for c in range(8):
                    first = (c % 2) * HALF + t0
                    r = 32 * (c % 4)
                    nc.sync.dma_start(
                        out=out[c // 2, 0, first : first + n, :, :].rearrange("(u s) f g -> (s f) u g", s=2),
                        in_=res[r : r + 32, c // 4 : n : 2, :],
                    )

            pending.extend([s1, s2, s3, s4, s5, s6, s7])

        def weights():
            nc.vector.tensor_copy(out=w_perm[:].rearrange("p (t m b) -> p t m b", t=4, b=2), in_=w_raw[:].rearrange("p (m t b) -> p t m b", t=4, b=2))
            nc.vector.tensor_copy(out=ws_perm[:].rearrange("p (t m) -> p t m", t=4), in_=ws_raw[:].rearrange("p (m t) -> p t m", t=4))
            nc.vector.tensor_copy(out=bqf[:], in_=bq_raw[:])
            for h in range(2):
                nc.vector.tensor_reduce(out=pick[:, h : h + 1], in_=ident[:].rearrange("p (a s f) -> p s a f", s=2, f=F)[:, h, :, :], axis=AX.XY, op=ALU.add)

        scale_x_first()
        for i in range(-3, UNITS + 3):
            if ok(i):
                project(i)
                add_bias(i)
            if ok(i + 3):
                transpose_k(i + 3)
                copy_k(i + 3)
            if ok(i - 2):
                scores(i - 2)
                if i - 2 == UNITS - 1 or (i - 2) % 2 == 1:
                    extract(i - 2)
            if ok(i + 2) or ok(i):
                new_xq(i + 2)
            if ok(i + 2):
                transpose_x(i + 2)
                copy_x(i + 2)
            if ok(i - 1):
                weave(i - 1)
            if i % 2 == 0 and pending:
                pending.pop(0)()
            if i > -3 and ok(i + 3):
                scale_x(i + 3)
            if i == -2:
                weights()
            if ok(i + 1) or ok(i - 1):
                quant_xq(i + 1)
            if i % 2 == 0:
                if pending:
                    pending.pop(0)()
            elif ok(i - 1):
                quant_k((i - 1) // 2)
        while pending:
            pending.pop(0)()
